import numpy as np
import ml_dtypes


def mxq(x, axis, fmt="e4m3"):
    dtype, down = {"e4m3": (ml_dtypes.float8_e4m3fn, 7), "e5m2": (ml_dtypes.float8_e5m2, 14)}[fmt]
    v = np.moveaxis(np.asarray(x, np.float32).astype(ml_dtypes.bfloat16).astype(np.float64), axis, -1)
    blocks = v.reshape(v.shape[:-1] + (-1, 32))
    amax = np.abs(blocks).max(-1, keepdims=True)
    byte = np.maximum(np.where(amax > 0, np.frexp(amax)[1] - 1 + 127, 0) - down, 1)
    scale = np.exp2(byte - 127.0)
    codes = (blocks / scale).astype(np.float32).astype(dtype).astype(np.float64)
    return np.moveaxis((codes * scale).reshape(v.shape), -1, axis)


WIDE = False


def mx_kscale(k):
    if not WIDE:
        return np.ones(k)
    levels = np.array([10, -10, 5, -5, 0])
    a = np.random.permutation(np.resize(levels, k // 512 * 4)).reshape(k // 512, 4)
    idx = np.arange(k)
    return np.exp2(a[idx // 512, idx % 128 // 32])


BF16 = ml_dtypes.bfloat16


def bf(x):
    return np.asarray(x, np.float32).astype(BF16)


def f64(x):
    return np.asarray(x).astype(np.float64)


T, HS, WS, WT, WH, WW, NH, HD, VID_DIM, TXT_DIM, TXT_LEN = 4, 4, 8, 4, 4, 4, 8, 128, 512, 1536, 256
EPS = 1e-6
L_VID = T * HS * WS
N_WIN = (T // WT) * (HS // WH) * (WS // WW)
WIN_LEN = WT * WH * WW
INNER = NH * HD


def rmsnorm(x, gain):
    return x * (1.0 / np.sqrt(np.mean(x * x, axis=-1, keepdims=True) + EPS)) * gain


def window_partition(x):
    x = x.reshape(T // WT, WT, HS // WH, WH, WS // WW, WW, NH, HD)
    x = x.transpose(0, 2, 4, 1, 3, 5, 6, 7)
    return x.reshape(N_WIN, WIN_LEN, NH, HD)


def setup_inputs():
    s = mx_kscale(VID_DIM)
    return {
        "vid": bf(np.random.standard_normal((L_VID, VID_DIM)) * s),
        "Wqkv_vid": bf(np.random.standard_normal((VID_DIM, 3 * INNER)) / np.sqrt(VID_DIM) / s[:, None]),
        "bqkv_vid": bf(0.1 * np.random.standard_normal(3 * INNER)),
        "q_scale_vid": bf(1.0 + 0.1 * np.random.standard_normal(HD)),
        "k_scale_vid": bf(1.0 + 0.1 * np.random.standard_normal(HD)),
    }


def reference(vid, Wqkv_vid, bqkv_vid, q_scale_vid, k_scale_vid):
    qkv = ((mxq(f64(vid), 1, "e4m3") @ mxq(f64(Wqkv_vid), 0, "e4m3")) + f64(bqkv_vid)).reshape(L_VID, 3, NH, HD)
    q = rmsnorm(qkv[:, 0], f64(q_scale_vid))
    k = rmsnorm(qkv[:, 1], f64(k_scale_vid))
    return window_partition(q), window_partition(k), window_partition(qkv[:, 2])

@@ -1,0 +1,195 @@
+from contextlib import ExitStack
+
+import concourse.mybir as mybir
+from concourse.masks import make_identity
+
+F32 = mybir.dt.float32
+BF16 = mybir.dt.bfloat16
+U32 = mybir.dt.uint32
+U8 = mybir.dt.uint8
+FP8X4 = mybir.dt.float8_e4m3fn_x4
+ALU = mybir.AluOpType
+ACT = mybir.ActivationFunctionType
+
+P = 128
+PACK = 4
+K = P * PACK
+HEAD = 128
+HEADS = 8
+PART = HEADS * HEAD
+PARTS = 3
+NORMED_PARTS = 2
+CHUNK = 512
+CHUNKS = PARTS * PART // CHUNK
+CHUNKS_PER_PART = PART // CHUNK
+HEADS_PER_CHUNK = CHUNK // HEAD
+EPS = 1e-6
+
+WINDOWS = 2
+WINDOW_W = 4
+
+SCALAR_COLS = 352
+
+FLOPS = 2 * P * K * PARTS * PART
+
+
+def runs_of_four(rows_first, columns_first):
+    return (
+        columns_first.rearrange("p (g i) j -> p g j i", i=4),
+        rows_first.rearrange("p j (g i) -> p g j i", i=4),
+    )
+
+
+def tile_naswinattention_pa_s_kernel(
+    tc, vid, Wqkv_vid, bqkv_vid, q_scale_vid, k_scale_vid, out_0, out_1, out_2
+):
+    nc = tc.nc
+    out_rows = [o.rearrange("n p h f -> (n p) (h f)") for o in (out_0, out_1, out_2)]
+    w_rows = Wqkv_vid.rearrange("(p j) n -> p j n", j=PACK)
+    gain_rows = [q_scale_vid, k_scale_vid]
+
+    with ExitStack() as ctx:
+        keep = ctx.enter_context(tc.tile_pool(name="keep", bufs=1))
+        psum = ctx.enter_context(tc.psum_pool(name="psum", bufs=1))
+
+        vid_sb = keep.tile([P, K], BF16)
+        vid_grouped = keep.tile([P, P * PACK], BF16, align_bytes=64)
+        vid_codes = keep.tile([P, P], U32, align_bytes=64)
+        vid_scales = keep.tile([P, P], U8, align_bytes=64)
+        w_raw = keep.tile([P, CHUNKS, PACK, CHUNK], BF16)
+        w_grouped = keep.tile([P, CHUNKS, CHUNK, PACK], BF16, align_bytes=64)
+        w_codes = keep.tile([P, CHUNKS, CHUNK], U32, align_bytes=64)
+        w_scales = keep.tile([P, CHUNKS, CHUNK], U8, align_bytes=64)
+        bias = keep.tile([P, CHUNKS, CHUNK], BF16)
+        gains = keep.tile([P, NORMED_PARTS, HEAD], BF16)
+        qkv = keep.tile([P, CHUNKS, CHUNK], F32)
+        squares = keep.tile([P, NORMED_PARTS * PART], F32)
+        normed = keep.tile([P, NORMED_PARTS * CHUNKS_PER_PART, CHUNK], F32)
+        sum_squares = keep.tile([P, NORMED_PARTS * HEADS], F32)
+        rms = keep.tile([P, NORMED_PARTS * HEADS], F32)
+        inv_rms = keep.tile([P, NORMED_PARTS * HEADS], F32)
+        eps = keep.tile([P, 1], F32)
+        table_warm = keep.tile([P, 1], F32)
+        identity = keep.tile([P, P], F32)
+        to_windows = keep.tile([P, P], F32)
+
+        nc.sync.dma_start(out=w_raw[:, 0], in_=w_rows[:, :, 0:CHUNK])
+        nc.sync.dma_start(out=vid_sb[:], in_=vid)
+        for c in range(1, CHUNKS):
+            nc.sync.dma_start(out=w_raw[:, c], in_=w_rows[:, :, c * CHUNK : (c + 1) * CHUNK])
+            if c % CHUNKS_PER_PART == CHUNKS_PER_PART - 1:
+                part = c // CHUNKS_PER_PART
+                nc.sync.dma_start(
+                    out=bias[:, part * CHUNKS_PER_PART : (part + 1) * CHUNKS_PER_PART, :].rearrange(
+                        "p c w -> p (c w)"
+                    ),
+                    in_=bqkv_vid[part * PART : (part + 1) * PART].partition_broadcast(P),
+                )
+                if part < NORMED_PARTS:
+                    nc.sync.dma_start(
+                        out=gains[:, part, :], in_=gain_rows[part].partition_broadcast(P)
+                    )
+
+        nc.vector.memset(eps[:], EPS)
+        nc.scalar.activation(out=table_warm[:], in_=eps[:], func=ACT.Sqrt)
+        make_identity(nc, identity[:])
+        nc.vector.tensor_copy(
+            out=to_windows[:].rearrange("l (n r c) -> l n r c", n=WINDOWS, c=WINDOW_W),
+            in_=identity[:].rearrange("l (r n c) -> l n r c", n=WINDOWS, c=WINDOW_W),
+        )
+
+        vid_words = vid_sb[:].bitcast(F32).rearrange("l (p u) -> l u p", u=2)
+        vid_t = psum.tile([P, 2, P], F32)
+        for u in range(2):
+            nc.tensor.transpose(vid_t[:, u, :], vid_words[:, u, :], to_windows[:])
+        nc.vector.tensor_copy(
+            out=vid_grouped[:].bitcast(F32).rearrange("p (l u) -> p l u", u=2),
+            in_=vid_t[:].rearrange("p u l -> p l u"),
+        )
+        nc.vector.quantize_mx(
+            out=vid_codes[:].bitcast(FP8X4), scales=vid_scales[:], in_=vid_grouped[:]
+        )
+
+        def regroup(c):
+            dst, src = runs_of_four(
+                w_raw[:, c, :, 0:SCALAR_COLS], w_grouped[:, c, 0:SCALAR_COLS, :]
+            )
+            nc.scalar.copy(out=dst, in_=src)
+            dst, src = runs_of_four(
+                w_raw[:, c, :, SCALAR_COLS:CHUNK], w_grouped[:, c, SCALAR_COLS:CHUNK, :]
+            )
+            nc.vector.tensor_copy(out=dst, in_=src)
+
+        def quantise(c):
+            nc.vector.quantize_mx(
+                out=w_codes[:, c, :].bitcast(FP8X4),
+                scales=w_scales[:, c, :],
+                in_=w_grouped[:, c].rearrange("p w j -> p (w j)"),
+            )
+
+        def project(c):
+            acc = psum.tile([P, CHUNK], F32, name="acc%d" % c)
+            nc.tensor.matmul_mx(
+                out=acc[:],
+                lhsT=vid_codes[:].bitcast(FP8X4),
+                lhsT_scale=vid_scales[:],
+                rhs=w_codes[:, c, :].bitcast(FP8X4),
+                rhs_scale=w_scales[:, c, :],
+                start=True,
+                stop=True,
+            )
+            nc.vector.tensor_tensor(out=qkv[:, c, :], in0=acc[:], in1=bias[:, c, :], op=ALU.add)
+
+        def store(c, result):
+            part = c // CHUNKS_PER_PART
+            first = (c % CHUNKS_PER_PART) * CHUNK
+            nc.sync.dma_start(out=out_rows[part][:, first : first + CHUNK], in_=result)
+
+        def measure(c):
+            heads = slice(c * HEADS_PER_CHUNK, (c + 1) * HEADS_PER_CHUNK)
+            for h in range(HEADS_PER_CHUNK):
+                head = c * HEADS_PER_CHUNK + h
+                nc.scalar.activation(
+                    out=squares[:, head * HEAD : (head + 1) * HEAD],
+                    in_=qkv[:, c, h * HEAD : (h + 1) * HEAD],
+                    func=ACT.Square,
+                    accum_out=sum_squares[:, head : head + 1],
+                )
+            nc.scalar.activation(
+                out=rms[:, heads],
+                in_=sum_squares[:, heads],
+                func=ACT.Sqrt,
+                bias=eps[:],
+                scale=1.0 / HEAD,
+            )
+
+        def normalise(c):
+            heads = slice(c * HEADS_PER_CHUNK, (c + 1) * HEADS_PER_CHUNK)
+            nc.vector.reciprocal(out=inv_rms[:, heads], in_=rms[:, heads])
+            for h in range(HEADS_PER_CHUNK):
+                head = c * HEADS_PER_CHUNK + h
+                features = slice(h * HEAD, (h + 1) * HEAD)
+                nc.vector.scalar_tensor_tensor(
+                    out=normed[:, c, features],
+                    in0=qkv[:, c, features],
+                    scalar=inv_rms[:, head : head + 1],
+                    in1=gains[:, c // CHUNKS_PER_PART, :],
+                    op0=ALU.mult,
+                    op1=ALU.mult,
+                )
+
+        normed_chunks = NORMED_PARTS * CHUNKS_PER_PART
+        for step in range(CHUNKS + 3):
+            if step < CHUNKS:
+                regroup(step)
+            if 0 <= step - 1 < CHUNKS:
+                quantise(step - 1)
+            if 0 <= step - 2 < CHUNKS:
+                project(step - 2)
+                if step - 2 < normed_chunks:
+                    measure(step - 2)
+                else:
+                    store(step - 2, qkv[:, step - 2, :])
+            if 0 <= step - 3 < normed_chunks:
+                normalise(step - 3)
+                store(step - 3, normed[:, step - 3, :])

@@ -28,6 +28,8 @@ EPS = 1e-6
 WINDOWS = 2
 WINDOW_W = 4
 
+BIAS_ROWS = PARTS * PART // HEAD
+
 SCALAR_COLS = 352
 
 FLOPS = 2 * P * K * PARTS * PART
@@ -60,7 +62,9 @@ def tile_naswinattention_pa_s_kernel(
         w_grouped = keep.tile([P, CHUNKS, CHUNK, PACK], BF16, align_bytes=64)
         w_codes = keep.tile([P, CHUNKS, CHUNK], U32, align_bytes=64)
         w_scales = keep.tile([P, CHUNKS, CHUNK], U8, align_bytes=64)
-        bias = keep.tile([P, CHUNKS, CHUNK], BF16)
+        vector_rows = keep.tile([P, P], BF16)
+        vector_columns = keep.tile([P, P], BF16)
+        bias = keep.tile([P, PARTS, PART], BF16)
         gains = keep.tile([P, NORMED_PARTS, HEAD], BF16)
         qkv = keep.tile([P, CHUNKS, CHUNK], F32)
         squares = keep.tile([P, NORMED_PARTS * PART], F32)
@@ -71,24 +75,22 @@ def tile_naswinattention_pa_s_kernel(
         eps = keep.tile([P, 1], F32)
         table_warm = keep.tile([P, 1], F32)
         identity = keep.tile([P, P], F32)
+        identity_bf = keep.tile([P, P], BF16)
         to_windows = keep.tile([P, P], F32)
 
         nc.sync.dma_start(out=w_raw[:, 0], in_=w_rows[:, :, 0:CHUNK])
         nc.sync.dma_start(out=vid_sb[:], in_=vid)
         for c in range(1, CHUNKS):
             nc.sync.dma_start(out=w_raw[:, c], in_=w_rows[:, :, c * CHUNK : (c + 1) * CHUNK])
-            if c % CHUNKS_PER_PART == CHUNKS_PER_PART - 1:
-                part = c // CHUNKS_PER_PART
-                nc.sync.dma_start(
-                    out=bias[:, part * CHUNKS_PER_PART : (part + 1) * CHUNKS_PER_PART, :].rearrange(
-                        "p c w -> p (c w)"
-                    ),
-                    in_=bqkv_vid[part * PART : (part + 1) * PART].partition_broadcast(P),
-                )
-                if part < NORMED_PARTS:
-                    nc.sync.dma_start(
-                        out=gains[:, part, :], in_=gain_rows[part].partition_broadcast(P)
-                    )
+        nc.vector.memset(vector_rows[:], 0.0)
+        nc.scalar.dma_start(
+            out=vector_rows[0:BIAS_ROWS, :], in_=bqkv_vid.rearrange("(m f) -> m f", f=HEAD)
+        )
+        for part in range(NORMED_PARTS):
+            nc.scalar.dma_start(
+                out=vector_rows[BIAS_ROWS + part : BIAS_ROWS + part + 1, :],
+                in_=gain_rows[part].rearrange("(o f) -> o f", o=1),
+            )
 
         nc.vector.memset(eps[:], EPS)
         nc.scalar.activation(out=table_warm[:], in_=eps[:], func=ACT.Sqrt)
@@ -98,8 +100,27 @@ def tile_naswinattention_pa_s_kernel(
             in_=identity[:].rearrange("l (r n c) -> l n r c", n=WINDOWS, c=WINDOW_W),
         )
 
+        make_identity(nc, identity_bf[:])
+        columns_ps = psum.tile([P, P], BF16, tag="bank7")
+        nc.tensor.transpose(columns_ps[:], vector_rows[:], identity_bf[:])
+        nc.vector.tensor_copy(out=vector_columns[:], in_=columns_ps[:])
+
+        def spread(first_row, rows, bank, result):
+            spread_ps = psum.tile([P, rows * HEAD], BF16, name="spread%d" % bank, tag="bank%d" % bank)
+            for m in range(rows):
+                nc.tensor.transpose(
+                    spread_ps[:, m * HEAD : (m + 1) * HEAD],
+                    vector_columns[:, first_row + m : first_row + m + 1].to_broadcast([P, P]),
+                    identity_bf[:],
+                )
+            nc.scalar.copy(out=result, in_=spread_ps[:])
+
+        for part in range(PARTS):
+            spread(part * HEADS, HEADS, part, bias[:, part, :])
+        spread(BIAS_ROWS, NORMED_PARTS, PARTS, gains[:].rearrange("p g f -> p (g f)"))
+
         vid_words = vid_sb[:].bitcast(F32).rearrange("l (p u) -> l u p", u=2)
-        vid_t = psum.tile([P, 2, P], F32)
+        vid_t = psum.tile([P, 2, P], F32, tag="bank6")
         for u in range(2):
             nc.tensor.transpose(vid_t[:, u, :], vid_words[:, u, :], to_windows[:])
         nc.vector.tensor_copy(
@@ -128,7 +149,7 @@ def tile_naswinattention_pa_s_kernel(
             )
 
         def project(c):
-            acc = psum.tile([P, CHUNK], F32, name="acc%d" % c)
+            acc = psum.tile([P, CHUNK], F32, name="acc%d" % c, tag="bank%d" % c)
             nc.tensor.matmul_mx(
                 out=acc[:],
                 lhsT=vid_codes[:].bitcast(FP8X4),
@@ -138,7 +159,12 @@ def tile_naswinattention_pa_s_kernel(
                 start=True,
                 stop=True,
             )
-            nc.vector.tensor_tensor(out=qkv[:, c, :], in0=acc[:], in1=bias[:, c, :], op=ALU.add)
+            nc.vector.tensor_tensor(
+                out=qkv[:, c, :],
+                in0=acc[:],
+                in1=bias[:].rearrange("p q (c w) -> p (q c) w", w=CHUNK)[:, c, :],
+                op=ALU.add,
+            )
 
         def store(c, result):
             part = c // CHUNKS_PER_PART

@@ -28,9 +28,9 @@ EPS = 1e-6
 WINDOWS = 2
 WINDOW_W = 4
 
-BIAS_ROWS = PARTS * PART // HEAD
-
-SCALAR_COLS = 352
+FILL_STEPS = 3
+SCALAR_COLS_FILLING = 240
+SCALAR_COLS = 336
 
 FLOPS = 2 * P * K * PARTS * PART
 
@@ -62,9 +62,7 @@ def tile_naswinattention_pa_s_kernel(
         w_grouped = keep.tile([P, CHUNKS, CHUNK, PACK], BF16, align_bytes=64)
         w_codes = keep.tile([P, CHUNKS, CHUNK], U32, align_bytes=64)
         w_scales = keep.tile([P, CHUNKS, CHUNK], U8, align_bytes=64)
-        vector_rows = keep.tile([P, P], BF16)
-        vector_columns = keep.tile([P, P], BF16)
-        bias = keep.tile([P, PARTS, PART], BF16)
+        bias = keep.tile([P, CHUNKS, CHUNK], BF16)
         gains = keep.tile([P, NORMED_PARTS, HEAD], BF16)
         qkv = keep.tile([P, CHUNKS, CHUNK], F32)
         squares = keep.tile([P, NORMED_PARTS * PART], F32)
@@ -75,22 +73,31 @@ def tile_naswinattention_pa_s_kernel(
         eps = keep.tile([P, 1], F32)
         table_warm = keep.tile([P, 1], F32)
         identity = keep.tile([P, P], F32)
-        identity_bf = keep.tile([P, P], BF16)
         to_windows = keep.tile([P, P], F32)
 
-        nc.sync.dma_start(out=w_raw[:, 0], in_=w_rows[:, :, 0:CHUNK])
-        nc.sync.dma_start(out=vid_sb[:], in_=vid)
-        for c in range(1, CHUNKS):
-            nc.sync.dma_start(out=w_raw[:, c], in_=w_rows[:, :, c * CHUNK : (c + 1) * CHUNK])
-        nc.vector.memset(vector_rows[:], 0.0)
-        nc.scalar.dma_start(
-            out=vector_rows[0:BIAS_ROWS, :], in_=bqkv_vid.rearrange("(m f) -> m f", f=HEAD)
-        )
-        for part in range(NORMED_PARTS):
-            nc.scalar.dma_start(
-                out=vector_rows[BIAS_ROWS + part : BIAS_ROWS + part + 1, :],
-                in_=gain_rows[part].rearrange("(o f) -> o f", o=1),
+        ctx.enter_context(tc.manual_schedule())
+
+        row_loads = []
+        for part in range(PARTS):
+            row_loads.append(
+                (
+                    bias[:, part * CHUNKS_PER_PART : (part + 1) * CHUNKS_PER_PART, :].rearrange(
+                        "p c w -> p (c w)"
+                    ),
+                    bqkv_vid[part * PART : (part + 1) * PART],
+                )
             )
+            if part < NORMED_PARTS:
+                row_loads.append((gains[:, part, :], gain_rows[part]))
+        for c in range(CHUNKS):
+            nc.sync.dma_start(out=w_raw[:, c], in_=w_rows[:, :, c * CHUNK : (c + 1) * CHUNK])
+            if c == 0:
+                nc.sync.dma_start(out=vid_sb[:], in_=vid)
+            if c >= 2:
+                rows_sb, row = row_loads[c - 2]
+                nc.sync.dma_start(out=rows_sb, in_=row.partition_broadcast(P))
+        for rows_sb, row in row_loads[CHUNKS - 2 :]:
+            nc.sync.dma_start(out=rows_sb, in_=row.partition_broadcast(P))
 
         nc.vector.memset(eps[:], EPS)
         nc.scalar.activation(out=table_warm[:], in_=eps[:], func=ACT.Sqrt)
@@ -100,45 +107,24 @@ def tile_naswinattention_pa_s_kernel(
             in_=identity[:].rearrange("l (r n c) -> l n r c", n=WINDOWS, c=WINDOW_W),
         )
 
-        make_identity(nc, identity_bf[:])
-        columns_ps = psum.tile([P, P], BF16, tag="bank7")
-        nc.tensor.transpose(columns_ps[:], vector_rows[:], identity_bf[:])
-        nc.vector.tensor_copy(out=vector_columns[:], in_=columns_ps[:])
-
-        def spread(first_row, rows, bank, result):
-            spread_ps = psum.tile([P, rows * HEAD], BF16, name="spread%d" % bank, tag="bank%d" % bank)
-            for m in range(rows):
-                nc.tensor.transpose(
-                    spread_ps[:, m * HEAD : (m + 1) * HEAD],
-                    vector_columns[:, first_row + m : first_row + m + 1].to_broadcast([P, P]),
-                    identity_bf[:],
-                )
-            nc.scalar.copy(out=result, in_=spread_ps[:])
-
-        for part in range(PARTS):
-            spread(part * HEADS, HEADS, part, bias[:, part, :])
-        spread(BIAS_ROWS, NORMED_PARTS, PARTS, gains[:].rearrange("p g f -> p (g f)"))
-
-        vid_words = vid_sb[:].bitcast(F32).rearrange("l (p u) -> l u p", u=2)
-        vid_t = psum.tile([P, 2, P], F32, tag="bank6")
-        for u in range(2):
-            nc.tensor.transpose(vid_t[:, u, :], vid_words[:, u, :], to_windows[:])
-        nc.vector.tensor_copy(
-            out=vid_grouped[:].bitcast(F32).rearrange("p (l u) -> p l u", u=2),
-            in_=vid_t[:].rearrange("p u l -> p l u"),
-        )
-        nc.vector.quantize_mx(
-            out=vid_codes[:].bitcast(FP8X4), scales=vid_scales[:], in_=vid_grouped[:]
-        )
+        def quantise_vid():
+            vid_words = vid_sb[:].bitcast(F32).rearrange("l (p u) -> l u p", u=2)
+            vid_t = psum.tile([P, 2, P], F32)
+            for u in range(2):
+                nc.tensor.transpose(vid_t[:, u, :], vid_words[:, u, :], to_windows[:])
+            nc.vector.tensor_copy(
+                out=vid_grouped[:].bitcast(F32).rearrange("p (l u) -> p l u", u=2),
+                in_=vid_t[:].rearrange("p u l -> p l u"),
+            )
+            nc.vector.quantize_mx(
+                out=vid_codes[:].bitcast(FP8X4), scales=vid_scales[:], in_=vid_grouped[:]
+            )
 
         def regroup(c):
-            dst, src = runs_of_four(
-                w_raw[:, c, :, 0:SCALAR_COLS], w_grouped[:, c, 0:SCALAR_COLS, :]
-            )
+            split = SCALAR_COLS_FILLING if c < FILL_STEPS else SCALAR_COLS
+            dst, src = runs_of_four(w_raw[:, c, :, 0:split], w_grouped[:, c, 0:split, :])
             nc.scalar.copy(out=dst, in_=src)
-            dst, src = runs_of_four(
-                w_raw[:, c, :, SCALAR_COLS:CHUNK], w_grouped[:, c, SCALAR_COLS:CHUNK, :]
-            )
+            dst, src = runs_of_four(w_raw[:, c, :, split:CHUNK], w_grouped[:, c, split:CHUNK, :])
             nc.vector.tensor_copy(out=dst, in_=src)
 
         def quantise(c):
@@ -148,10 +134,11 @@ def tile_naswinattention_pa_s_kernel(
                 in_=w_grouped[:, c].rearrange("p w j -> p (w j)"),
             )
 
+        accs = [psum.tile([P, CHUNK], F32, name="acc%d" % c) for c in range(CHUNKS)]
+
         def project(c):
-            acc = psum.tile([P, CHUNK], F32, name="acc%d" % c, tag="bank%d" % c)
             nc.tensor.matmul_mx(
-                out=acc[:],
+                out=accs[c][:],
                 lhsT=vid_codes[:].bitcast(FP8X4),
                 lhsT_scale=vid_scales[:],
                 rhs=w_codes[:, c, :].bitcast(FP8X4),
@@ -159,11 +146,10 @@ def tile_naswinattention_pa_s_kernel(
                 start=True,
                 stop=True,
             )
+
+        def add_bias(c):
             nc.vector.tensor_tensor(
-                out=qkv[:, c, :],
-                in0=acc[:],
-                in1=bias[:].rearrange("p q (c w) -> p (q c) w", w=CHUNK)[:, c, :],
-                op=ALU.add,
+                out=qkv[:, c, :], in0=accs[c][:], in1=bias[:, c, :], op=ALU.add
             )
 
         def store(c, result):
@@ -171,8 +157,7 @@ def tile_naswinattention_pa_s_kernel(
             first = (c % CHUNKS_PER_PART) * CHUNK
             nc.sync.dma_start(out=out_rows[part][:, first : first + CHUNK], in_=result)
 
-        def measure(c):
-            heads = slice(c * HEADS_PER_CHUNK, (c + 1) * HEADS_PER_CHUNK)
+        def sum_the_squares(c):
             for h in range(HEADS_PER_CHUNK):
                 head = c * HEADS_PER_CHUNK + h
                 nc.scalar.activation(
@@ -181,6 +166,9 @@ def tile_naswinattention_pa_s_kernel(
                     func=ACT.Square,
                     accum_out=sum_squares[:, head : head + 1],
                 )
+
+        def root(c):
+            heads = slice(c * HEADS_PER_CHUNK, (c + 1) * HEADS_PER_CHUNK)
             nc.scalar.activation(
                 out=rms[:, heads],
                 in_=sum_squares[:, heads],
@@ -206,14 +194,19 @@ def tile_naswinattention_pa_s_kernel(
 
         normed_chunks = NORMED_PARTS * CHUNKS_PER_PART
         for step in range(CHUNKS + 3):
+            if 0 <= step - 3 < normed_chunks:
+                root(step - 3)
             if step < CHUNKS:
                 regroup(step)
+            if step == 0:
+                quantise_vid()
             if 0 <= step - 1 < CHUNKS:
                 quantise(step - 1)
+                project(step - 1)
             if 0 <= step - 2 < CHUNKS:
-                project(step - 2)
+                add_bias(step - 2)
                 if step - 2 < normed_chunks:
-                    measure(step - 2)
+                    sum_the_squares(step - 2)
                 else:
                     store(step - 2, qkv[:, step - 2, :])
             if 0 <= step - 3 < normed_chunks:

@@ -28,9 +28,7 @@ EPS = 1e-6
 WINDOWS = 2
 WINDOW_W = 4
 
-FILL_STEPS = 3
-SCALAR_COLS_FILLING = 240
-SCALAR_COLS = 336
+SCALAR_COLS = 272
 
 FLOPS = 2 * P * K * PARTS * PART
 
@@ -121,10 +119,13 @@ def tile_naswinattention_pa_s_kernel(
             )
 
         def regroup(c):
-            split = SCALAR_COLS_FILLING if c < FILL_STEPS else SCALAR_COLS
-            dst, src = runs_of_four(w_raw[:, c, :, 0:split], w_grouped[:, c, 0:split, :])
+            dst, src = runs_of_four(
+                w_raw[:, c, :, 0:SCALAR_COLS], w_grouped[:, c, 0:SCALAR_COLS, :]
+            )
             nc.scalar.copy(out=dst, in_=src)
-            dst, src = runs_of_four(w_raw[:, c, :, split:CHUNK], w_grouped[:, c, split:CHUNK, :])
+            dst, src = runs_of_four(
+                w_raw[:, c, :, SCALAR_COLS:CHUNK], w_grouped[:, c, SCALAR_COLS:CHUNK, :]
+            )
             nc.vector.tensor_copy(out=dst, in_=src)
 
         def quantise(c):
@@ -196,13 +197,13 @@ def tile_naswinattention_pa_s_kernel(
         for step in range(CHUNKS + 3):
             if 0 <= step - 3 < normed_chunks:
                 root(step - 3)
+            if 0 <= step - 1 < CHUNKS:
+                quantise(step - 1)
+                project(step - 1)
             if step < CHUNKS:
                 regroup(step)
             if step == 0:
                 quantise_vid()
-            if 0 <= step - 1 < CHUNKS:
-                quantise(step - 1)
-                project(step - 1)
             if 0 <= step - 2 < CHUNKS:
                 add_bias(step - 2)
                 if step - 2 < normed_chunks:

@@ -178,9 +178,11 @@ def tile_naswinattention_pa_s_kernel(
                 scale=1.0 / HEAD,
             )
 
-        def normalise(c):
+        def invert(c):
             heads = slice(c * HEADS_PER_CHUNK, (c + 1) * HEADS_PER_CHUNK)
             nc.vector.reciprocal(out=inv_rms[:, heads], in_=rms[:, heads])
+
+        def normalise(c):
             for h in range(HEADS_PER_CHUNK):
                 head = c * HEADS_PER_CHUNK + h
                 features = slice(h * HEAD, (h + 1) * HEAD)
@@ -194,9 +196,7 @@ def tile_naswinattention_pa_s_kernel(
                 )
 
         normed_chunks = NORMED_PARTS * CHUNKS_PER_PART
-        for step in range(CHUNKS + 3):
-            if 0 <= step - 3 < normed_chunks:
-                root(step - 3)
+        for step in range(CHUNKS + 4):
             if 0 <= step - 1 < CHUNKS:
                 quantise(step - 1)
                 project(step - 1)
@@ -204,12 +204,16 @@ def tile_naswinattention_pa_s_kernel(
                 regroup(step)
             if step == 0:
                 quantise_vid()
+            if 0 <= step - 3 < normed_chunks:
+                root(step - 3)
             if 0 <= step - 2 < CHUNKS:
                 add_bias(step - 2)
                 if step - 2 < normed_chunks:
                     sum_the_squares(step - 2)
                 else:
                     store(step - 2, qkv[:, step - 2, :])
+            if 0 <= step - 4 < normed_chunks:
+                normalise(step - 4)
+                store(step - 4, normed[:, step - 4, :])
             if 0 <= step - 3 < normed_chunks:
-                normalise(step - 3)
-                store(step - 3, normed[:, step - 3, :])
+                invert(step - 3)

@@ -28,7 +28,13 @@ EPS = 1e-6
 WINDOWS = 2
 WINDOW_W = 4
 
-SCALAR_COLS = 272
+SCALAR_COLS_FIRST = 240
+SCALAR_COLS_STEP = 32
+SCALAR_COLS_LAST = 368
+
+
+def scalar_cols(c):
+    return min(SCALAR_COLS_FIRST + SCALAR_COLS_STEP * c, SCALAR_COLS_LAST)
 
 FLOPS = 2 * P * K * PARTS * PART
 
@@ -66,7 +72,6 @@ def tile_naswinattention_pa_s_kernel(
         squares = keep.tile([P, NORMED_PARTS * PART], F32)
         normed = keep.tile([P, NORMED_PARTS * CHUNKS_PER_PART, CHUNK], F32)
         sum_squares = keep.tile([P, NORMED_PARTS * HEADS], F32)
-        rms = keep.tile([P, NORMED_PARTS * HEADS], F32)
         inv_rms = keep.tile([P, NORMED_PARTS * HEADS], F32)
         eps = keep.tile([P, 1], F32)
         table_warm = keep.tile([P, 1], F32)
@@ -98,7 +103,7 @@ def tile_naswinattention_pa_s_kernel(
             nc.sync.dma_start(out=rows_sb, in_=row.partition_broadcast(P))
 
         nc.vector.memset(eps[:], EPS)
-        nc.scalar.activation(out=table_warm[:], in_=eps[:], func=ACT.Sqrt)
+        nc.scalar.activation(out=table_warm[:], in_=eps[:], func=ACT.Abs_reciprocal_sqrt)
         make_identity(nc, identity[:])
         nc.vector.tensor_copy(
             out=to_windows[:].rearrange("l (n r c) -> l n r c", n=WINDOWS, c=WINDOW_W),
@@ -119,13 +124,10 @@ def tile_naswinattention_pa_s_kernel(
             )
 
         def regroup(c):
-            dst, src = runs_of_four(
-                w_raw[:, c, :, 0:SCALAR_COLS], w_grouped[:, c, 0:SCALAR_COLS, :]
-            )
+            cut = scalar_cols(c)
+            dst, src = runs_of_four(w_raw[:, c, :, 0:cut], w_grouped[:, c, 0:cut, :])
             nc.scalar.copy(out=dst, in_=src)
-            dst, src = runs_of_four(
-                w_raw[:, c, :, SCALAR_COLS:CHUNK], w_grouped[:, c, SCALAR_COLS:CHUNK, :]
-            )
+            dst, src = runs_of_four(w_raw[:, c, :, cut:CHUNK], w_grouped[:, c, cut:CHUNK, :])
             nc.vector.tensor_copy(out=dst, in_=src)
 
         def quantise(c):
@@ -171,16 +173,12 @@ def tile_naswinattention_pa_s_kernel(
         def root(c):
             heads = slice(c * HEADS_PER_CHUNK, (c + 1) * HEADS_PER_CHUNK)
             nc.scalar.activation(
-                out=rms[:, heads],
+                out=inv_rms[:, heads],
                 in_=sum_squares[:, heads],
-                func=ACT.Sqrt,
+                func=ACT.Abs_reciprocal_sqrt,
                 bias=eps[:],
                 scale=1.0 / HEAD,
             )
-
-        def invert(c):
-            heads = slice(c * HEADS_PER_CHUNK, (c + 1) * HEADS_PER_CHUNK)
-            nc.vector.reciprocal(out=inv_rms[:, heads], in_=rms[:, heads])
 
         def normalise(c):
             for h in range(HEADS_PER_CHUNK):
@@ -204,16 +202,13 @@ def tile_naswinattention_pa_s_kernel(
                 regroup(step)
             if step == 0:
                 quantise_vid()
-            if 0 <= step - 3 < normed_chunks:
-                root(step - 3)
             if 0 <= step - 2 < CHUNKS:
                 add_bias(step - 2)
-                if step - 2 < normed_chunks:
-                    sum_the_squares(step - 2)
-                else:
+                if step - 2 >= normed_chunks:
                     store(step - 2, qkv[:, step - 2, :])
+            if 0 <= step - 3 < normed_chunks:
+                sum_the_squares(step - 3)
+                root(step - 3)
             if 0 <= step - 4 < normed_chunks:
                 normalise(step - 4)
                 store(step - 4, normed[:, step - 4, :])
-            if 0 <= step - 3 < normed_chunks:
-                invert(step - 3)

@@ -80,30 +80,32 @@ def tile_naswinattention_pa_s_kernel(
 
         ctx.enter_context(tc.manual_schedule())
 
-        row_loads = []
-        for part in range(PARTS):
-            row_loads.append(
-                (
-                    bias[:, part * CHUNKS_PER_PART : (part + 1) * CHUNKS_PER_PART, :].rearrange(
-                        "p c w -> p (c w)"
-                    ),
-                    bqkv_vid[part * PART : (part + 1) * PART],
-                )
-            )
-            if part < NORMED_PARTS:
-                row_loads.append((gains[:, part, :], gain_rows[part]))
         for c in range(CHUNKS):
             nc.sync.dma_start(out=w_raw[:, c], in_=w_rows[:, :, c * CHUNK : (c + 1) * CHUNK])
             if c == 0:
                 nc.sync.dma_start(out=vid_sb[:], in_=vid)
-            if c >= 2:
-                rows_sb, row = row_loads[c - 2]
-                nc.sync.dma_start(out=rows_sb, in_=row.partition_broadcast(P))
-        for rows_sb, row in row_loads[CHUNKS - 2 :]:
-            nc.sync.dma_start(out=rows_sb, in_=row.partition_broadcast(P))
 
         nc.vector.memset(eps[:], EPS)
         nc.scalar.activation(out=table_warm[:], in_=eps[:], func=ACT.Abs_reciprocal_sqrt)
+
+        def bias_load(part):
+            nc.scalar.dma_start(
+                out=bias[:, part * CHUNKS_PER_PART : (part + 1) * CHUNKS_PER_PART, :].rearrange(
+                    "p c w -> p (c w)"
+                ),
+                in_=bqkv_vid[part * PART : (part + 1) * PART].partition_broadcast(P),
+            )
+
+        def gain_load(part):
+            nc.scalar.dma_start(
+                out=gains[:, part, :], in_=gain_rows[part].partition_broadcast(P)
+            )
+
+        bias_load(0)
+        bias_load(1)
+        gain_load(0)
+        bias_load(2)
+        gain_load(1)
         make_identity(nc, identity[:])
         nc.vector.tensor_copy(
             out=to_windows[:].rearrange("l (n r c) -> l n r c", n=WINDOWS, c=WINDOW_W),
@@ -194,7 +196,7 @@ def tile_naswinattention_pa_s_kernel(
                 )
 
         normed_chunks = NORMED_PARTS * CHUNKS_PER_PART
-        for step in range(CHUNKS + 4):
+        for step in range(CHUNKS + 3):
             if 0 <= step - 1 < CHUNKS:
                 quantise(step - 1)
                 project(step - 1)
@@ -202,13 +204,13 @@ def tile_naswinattention_pa_s_kernel(
                 regroup(step)
             if step == 0:
                 quantise_vid()
-            if 0 <= step - 2 < CHUNKS:
-                add_bias(step - 2)
-                if step - 2 >= normed_chunks:
-                    store(step - 2, qkv[:, step - 2, :])
-            if 0 <= step - 3 < normed_chunks:
-                sum_the_squares(step - 3)
-                root(step - 3)
+            if 0 <= step - 3 < CHUNKS:
+                add_bias(step - 3)
+                if step - 3 >= normed_chunks:
+                    store(step - 3, qkv[:, step - 3, :])
             if 0 <= step - 4 < normed_chunks:
-                normalise(step - 4)
-                store(step - 4, normed[:, step - 4, :])
+                sum_the_squares(step - 4)
+                root(step - 4)
+            if 0 <= step - 5 < normed_chunks:
+                normalise(step - 5)
+                store(step - 5, normed[:, step - 5, :])

@@ -88,8 +88,14 @@ def tile_naswinattention_pa_s_kernel(
         nc.vector.memset(eps[:], EPS)
         nc.scalar.activation(out=table_warm[:], in_=eps[:], func=ACT.Abs_reciprocal_sqrt)
 
+        make_identity(nc, identity[:])
+        nc.vector.tensor_copy(
+            out=to_windows[:].rearrange("l (n r c) -> l n r c", n=WINDOWS, c=WINDOW_W),
+            in_=identity[:].rearrange("l (r n c) -> l n r c", n=WINDOWS, c=WINDOW_W),
+        )
+
         def bias_load(part):
-            nc.scalar.dma_start(
+            nc.gpsimd.dma_start(
                 out=bias[:, part * CHUNKS_PER_PART : (part + 1) * CHUNKS_PER_PART, :].rearrange(
                     "p c w -> p (c w)"
                 ),
@@ -97,7 +103,7 @@ def tile_naswinattention_pa_s_kernel(
             )
 
         def gain_load(part):
-            nc.scalar.dma_start(
+            nc.gpsimd.dma_start(
                 out=gains[:, part, :], in_=gain_rows[part].partition_broadcast(P)
             )
 
@@ -106,11 +112,6 @@ def tile_naswinattention_pa_s_kernel(
         gain_load(0)
         bias_load(2)
         gain_load(1)
-        make_identity(nc, identity[:])
-        nc.vector.tensor_copy(
-            out=to_windows[:].rearrange("l (n r c) -> l n r c", n=WINDOWS, c=WINDOW_W),
-            in_=identity[:].rearrange("l (r n c) -> l n r c", n=WINDOWS, c=WINDOW_W),
-        )
 
         def quantise_vid():
             vid_words = vid_sb[:].bitcast(F32).rearrange("l (p u) -> l u p", u=2)

@@ -36,6 +36,10 @@ SCALAR_COLS_LAST = 368
 def scalar_cols(c):
     return min(SCALAR_COLS_FIRST + SCALAR_COLS_STEP * c, SCALAR_COLS_LAST)
 
+BIAS_ROWS = PARTS * HEADS
+USED_ROWS = 32
+FRESH_BANKS = 2
+
 FLOPS = 2 * P * K * PARTS * PART
 
 
@@ -67,7 +71,8 @@ def tile_naswinattention_pa_s_kernel(
         w_codes = keep.tile([P, CHUNKS, CHUNK], U32, align_bytes=64)
         w_scales = keep.tile([P, CHUNKS, CHUNK], U8, align_bytes=64)
         bias = keep.tile([P, CHUNKS, CHUNK], BF16)
-        gains = keep.tile([P, NORMED_PARTS, HEAD], BF16)
+        rows = keep.tile([P, HEAD], BF16)
+        columns = keep.tile([P, USED_ROWS], BF16)
         qkv = keep.tile([P, CHUNKS, CHUNK], F32)
         squares = keep.tile([P, NORMED_PARTS * PART], F32)
         normed = keep.tile([P, NORMED_PARTS * CHUNKS_PER_PART, CHUNK], F32)
@@ -77,12 +82,29 @@ def tile_naswinattention_pa_s_kernel(
         table_warm = keep.tile([P, 1], F32)
         identity = keep.tile([P, P], F32)
         to_windows = keep.tile([P, P], F32)
+        identity_bf = keep.tile([P, P], BF16)
+        accs = [psum.tile([P, CHUNK], F32, name="acc%d" % c) for c in range(FRESH_BANKS)]
+        columns_ps = psum.tile([P, P], BF16, name="acc%d" % FRESH_BANKS)
+        spread_bias = [
+            psum.tile([P, PART], BF16, name="acc%d" % (FRESH_BANKS + 1 + part))
+            for part in range(PARTS)
+        ]
+        gains = psum.tile([P, NORMED_PARTS, HEAD], BF16)
 
         ctx.enter_context(tc.manual_schedule())
 
+        nc.gpsimd.memset(rows[:], 0.0)
+        bias_rows = bqkv_vid.rearrange("(r f) -> r f", f=HEAD)
         for c in range(CHUNKS):
             nc.sync.dma_start(out=w_raw[:, c], in_=w_rows[:, :, c * CHUNK : (c + 1) * CHUNK])
             if c == 0:
+                nc.sync.dma_start(out=rows[0:16, :], in_=bias_rows[0:16, :])
+                nc.sync.dma_start(out=rows[16:BIAS_ROWS, :], in_=bias_rows[16:BIAS_ROWS, :])
+                for part in range(NORMED_PARTS):
+                    nc.sync.dma_start(
+                        out=rows[BIAS_ROWS + part : BIAS_ROWS + part + 1, :],
+                        in_=gain_rows[part].rearrange("(o f) -> o f", o=1),
+                    )
                 nc.sync.dma_start(out=vid_sb[:], in_=vid)
 
         nc.vector.memset(eps[:], EPS)
@@ -94,24 +116,30 @@ def tile_naswinattention_pa_s_kernel(
             in_=identity[:].rearrange("l (r n c) -> l n r c", n=WINDOWS, c=WINDOW_W),
         )
 
-        def bias_load(part):
-            nc.gpsimd.dma_start(
+        nc.vector.tensor_copy(out=identity_bf[:], in_=identity[:])
+
+        def rows_to_columns():
+            nc.tensor.transpose(columns_ps[:], rows[:], identity_bf[:])
+            nc.vector.tensor_copy(out=columns[:], in_=columns_ps[:, 0:USED_ROWS])
+
+        def spread(r, target):
+            nc.tensor.transpose(target, columns[:, r : r + 1].to_broadcast([P, P]), identity_bf[:])
+
+        def spread_bias_of(part):
+            for h in range(HEADS):
+                spread(part * HEADS + h, spread_bias[part][:, h * HEAD : (h + 1) * HEAD])
+
+        def spread_gains():
+            for part in range(NORMED_PARTS):
+                spread(BIAS_ROWS + part, gains[:, part, :])
+
+        def bias_to_sbuf(part):
+            nc.scalar.copy(
                 out=bias[:, part * CHUNKS_PER_PART : (part + 1) * CHUNKS_PER_PART, :].rearrange(
                     "p c w -> p (c w)"
                 ),
-                in_=bqkv_vid[part * PART : (part + 1) * PART].partition_broadcast(P),
+                in_=spread_bias[part][:],
             )
-
-        def gain_load(part):
-            nc.gpsimd.dma_start(
-                out=gains[:, part, :], in_=gain_rows[part].partition_broadcast(P)
-            )
-
-        bias_load(0)
-        bias_load(1)
-        gain_load(0)
-        bias_load(2)
-        gain_load(1)
 
         def quantise_vid():
             vid_words = vid_sb[:].bitcast(F32).rearrange("l (p u) -> l u p", u=2)
@@ -140,9 +168,9 @@ def tile_naswinattention_pa_s_kernel(
                 in_=w_grouped[:, c].rearrange("p w j -> p (w j)"),
             )
 
-        accs = [psum.tile([P, CHUNK], F32, name="acc%d" % c) for c in range(CHUNKS)]
-
         def project(c):
+            if c >= FRESH_BANKS:
+                accs.append(psum.tile([P, CHUNK], F32, name="acc%d" % c))
             nc.tensor.matmul_mx(
                 out=accs[c][:],
                 lhsT=vid_codes[:].bitcast(FP8X4),
@@ -204,7 +232,14 @@ def tile_naswinattention_pa_s_kernel(
             if step < CHUNKS:
                 regroup(step)
             if step == 0:
+                rows_to_columns()
                 quantise_vid()
+            if step < PARTS:
+                spread_bias_of(step)
+            if step == 1:
+                spread_gains()
+            if 0 <= step - 1 < PARTS:
+                bias_to_sbuf(step - 1)
             if 0 <= step - 3 < CHUNKS:
                 add_bias(step - 3)
                 if step - 3 >= normed_chunks:

@@ -28,16 +28,18 @@ EPS = 1e-6
 WINDOWS = 2
 WINDOW_W = 4
 
-SCALAR_COLS_FIRST = 240
+SCALAR_COLS_FIRST = 192
 SCALAR_COLS_STEP = 32
-SCALAR_COLS_LAST = 368
+SCALAR_COLS_LAST = 352
 
 
 def scalar_cols(c):
     return min(SCALAR_COLS_FIRST + SCALAR_COLS_STEP * c, SCALAR_COLS_LAST)
 
-BIAS_ROWS = PARTS * HEADS
-USED_ROWS = 32
+ROW = 2 * HEAD
+ROWS_PER_PART = PART // ROW
+BIAS_ROWS = PARTS * ROWS_PER_PART
+USED_ROWS = 16
 FRESH_BANKS = 2
 
 FLOPS = 2 * P * K * PARTS * PART
@@ -71,8 +73,8 @@ def tile_naswinattention_pa_s_kernel(
         w_codes = keep.tile([P, CHUNKS, CHUNK], U32, align_bytes=64)
         w_scales = keep.tile([P, CHUNKS, CHUNK], U8, align_bytes=64)
         bias = keep.tile([P, CHUNKS, CHUNK], BF16)
-        rows = keep.tile([P, HEAD], BF16)
-        columns = keep.tile([P, USED_ROWS], BF16)
+        rows = keep.tile([P, ROW], BF16)
+        columns = keep.tile([P, USED_ROWS], F32)
         qkv = keep.tile([P, CHUNKS, CHUNK], F32)
         squares = keep.tile([P, NORMED_PARTS * PART], F32)
         normed = keep.tile([P, NORMED_PARTS * CHUNKS_PER_PART, CHUNK], F32)
@@ -82,27 +84,27 @@ def tile_naswinattention_pa_s_kernel(
         table_warm = keep.tile([P, 1], F32)
         identity = keep.tile([P, P], F32)
         to_windows = keep.tile([P, P], F32)
-        identity_bf = keep.tile([P, P], BF16)
         accs = [psum.tile([P, CHUNK], F32, name="acc%d" % c) for c in range(FRESH_BANKS)]
-        columns_ps = psum.tile([P, P], BF16, name="acc%d" % FRESH_BANKS)
+        columns_ps = psum.tile([P, P], F32, name="acc%d" % FRESH_BANKS)
         spread_bias = [
-            psum.tile([P, PART], BF16, name="acc%d" % (FRESH_BANKS + 1 + part))
+            psum.tile([P, ROWS_PER_PART, P], F32, name="acc%d" % (FRESH_BANKS + 1 + part))
             for part in range(PARTS)
         ]
-        gains = psum.tile([P, NORMED_PARTS, HEAD], BF16)
+        gain_words = psum.tile([P, P], F32)
+        gains = gain_words[:].bitcast(BF16).rearrange("p (g f) -> p g f", g=NORMED_PARTS)
 
         ctx.enter_context(tc.manual_schedule())
 
         nc.gpsimd.memset(rows[:], 0.0)
-        bias_rows = bqkv_vid.rearrange("(r f) -> r f", f=HEAD)
+        bias_rows = bqkv_vid.rearrange("(r f) -> r f", f=ROW)
         for c in range(CHUNKS):
             nc.sync.dma_start(out=w_raw[:, c], in_=w_rows[:, :, c * CHUNK : (c + 1) * CHUNK])
             if c == 0:
-                nc.sync.dma_start(out=rows[0:16, :], in_=bias_rows[0:16, :])
-                nc.sync.dma_start(out=rows[16:BIAS_ROWS, :], in_=bias_rows[16:BIAS_ROWS, :])
+                nc.sync.dma_start(out=rows[0:8, :], in_=bias_rows[0:8, :])
+                nc.sync.dma_start(out=rows[8:BIAS_ROWS, :], in_=bias_rows[8:BIAS_ROWS, :])
                 for part in range(NORMED_PARTS):
                     nc.sync.dma_start(
-                        out=rows[BIAS_ROWS + part : BIAS_ROWS + part + 1, :],
+                        out=rows[BIAS_ROWS : BIAS_ROWS + 1, part * HEAD : (part + 1) * HEAD],
                         in_=gain_rows[part].rearrange("(o f) -> o f", o=1),
                     )
                 nc.sync.dma_start(out=vid_sb[:], in_=vid)
@@ -116,29 +118,26 @@ def tile_naswinattention_pa_s_kernel(
             in_=identity[:].rearrange("l (r n c) -> l n r c", n=WINDOWS, c=WINDOW_W),
         )
 
-        nc.vector.tensor_copy(out=identity_bf[:], in_=identity[:])
-
         def rows_to_columns():
-            nc.tensor.transpose(columns_ps[:], rows[:], identity_bf[:])
+            nc.tensor.transpose(columns_ps[:], rows[:].bitcast(F32), identity[:])
             nc.vector.tensor_copy(out=columns[:], in_=columns_ps[:, 0:USED_ROWS])
 
         def spread(r, target):
-            nc.tensor.transpose(target, columns[:, r : r + 1].to_broadcast([P, P]), identity_bf[:])
+            nc.tensor.transpose(target, columns[:, r : r + 1].to_broadcast([P, P]), identity[:])
 
         def spread_bias_of(part):
-            for h in range(HEADS):
-                spread(part * HEADS + h, spread_bias[part][:, h * HEAD : (h + 1) * HEAD])
+            for i in range(ROWS_PER_PART):
+                spread(part * ROWS_PER_PART + i, spread_bias[part][:, i, :])
 
         def spread_gains():
-            for part in range(NORMED_PARTS):
-                spread(BIAS_ROWS + part, gains[:, part, :])
+            spread(BIAS_ROWS, gain_words[:])
 
         def bias_to_sbuf(part):
             nc.scalar.copy(
-                out=bias[:, part * CHUNKS_PER_PART : (part + 1) * CHUNKS_PER_PART, :].rearrange(
-                    "p c w -> p (c w)"
-                ),
-                in_=spread_bias[part][:],
+                out=bias[:, part * CHUNKS_PER_PART : (part + 1) * CHUNKS_PER_PART, :]
+                .rearrange("p c w -> p (c w)")
+                .bitcast(F32),
+                in_=spread_bias[part][:].rearrange("p i w -> p (i w)"),
             )
 
         def quantise_vid():
@@ -238,8 +237,8 @@ def tile_naswinattention_pa_s_kernel(
                 spread_bias_of(step)
             if step == 1:
                 spread_gains()
-            if 0 <= step - 1 < PARTS:
-                bias_to_sbuf(step - 1)
+            if 0 <= step - 2 < PARTS:
+                bias_to_sbuf(step - 2)
             if 0 <= step - 3 < CHUNKS:
                 add_bias(step - 3)
                 if step - 3 >= normed_chunks:

@@ -38,7 +38,7 @@ def scalar_cols(c):
 
 ROW = 2 * HEAD
 ROWS_PER_PART = PART // ROW
-BIAS_ROWS = PARTS * ROWS_PER_PART
+BIAS_ROWS = NORMED_PARTS * ROWS_PER_PART
 USED_ROWS = 16
 FRESH_BANKS = 2
 
@@ -88,7 +88,7 @@ def tile_naswinattention_pa_s_kernel(
         columns_ps = psum.tile([P, P], F32, name="acc%d" % FRESH_BANKS)
         spread_bias = [
             psum.tile([P, ROWS_PER_PART, P], F32, name="acc%d" % (FRESH_BANKS + 1 + part))
-            for part in range(PARTS)
+            for part in range(NORMED_PARTS)
         ]
         gain_words = psum.tile([P, P], F32)
         gains = gain_words[:].bitcast(BF16).rearrange("p (g f) -> p g f", g=NORMED_PARTS)
@@ -100,14 +100,17 @@ def tile_naswinattention_pa_s_kernel(
         for c in range(CHUNKS):
             nc.sync.dma_start(out=w_raw[:, c], in_=w_rows[:, :, c * CHUNK : (c + 1) * CHUNK])
             if c == 0:
-                nc.sync.dma_start(out=rows[0:8, :], in_=bias_rows[0:8, :])
-                nc.sync.dma_start(out=rows[8:BIAS_ROWS, :], in_=bias_rows[8:BIAS_ROWS, :])
+                nc.sync.dma_start(out=rows[0:BIAS_ROWS, :], in_=bias_rows[0:BIAS_ROWS, :])
                 for part in range(NORMED_PARTS):
                     nc.sync.dma_start(
                         out=rows[BIAS_ROWS : BIAS_ROWS + 1, part * HEAD : (part + 1) * HEAD],
                         in_=gain_rows[part].rearrange("(o f) -> o f", o=1),
                     )
                 nc.sync.dma_start(out=vid_sb[:], in_=vid)
+        nc.sync.dma_start(
+            out=bias[:, NORMED_PARTS * CHUNKS_PER_PART : CHUNKS, :].rearrange("p c w -> p (c w)"),
+            in_=bqkv_vid[NORMED_PARTS * PART : PARTS * PART].partition_broadcast(P),
+        )
 
         nc.vector.memset(eps[:], EPS)
         nc.scalar.activation(out=table_warm[:], in_=eps[:], func=ACT.Abs_reciprocal_sqrt)
@@ -233,11 +236,10 @@ def tile_naswinattention_pa_s_kernel(
             if step == 0:
                 rows_to_columns()
                 quantise_vid()
-            if step < PARTS:
-                spread_bias_of(step)
-            if step == 1:
+                for part in range(NORMED_PARTS):
+                    spread_bias_of(part)
                 spread_gains()
-            if 0 <= step - 2 < PARTS:
+            if 0 <= step - 2 < NORMED_PARTS:
                 bias_to_sbuf(step - 2)
             if 0 <= step - 3 < CHUNKS:
                 add_bias(step - 3)

@@ -227,7 +227,7 @@ def tile_naswinattention_pa_s_kernel(
                 )
 
         normed_chunks = NORMED_PARTS * CHUNKS_PER_PART
-        for step in range(CHUNKS + 3):
+        for step in range(CHUNKS + 2):
             if 0 <= step - 1 < CHUNKS:
                 quantise(step - 1)
                 project(step - 1)
@@ -239,15 +239,15 @@ def tile_naswinattention_pa_s_kernel(
                 for part in range(NORMED_PARTS):
                     spread_bias_of(part)
                 spread_gains()
-            if 0 <= step - 2 < NORMED_PARTS:
-                bias_to_sbuf(step - 2)
-            if 0 <= step - 3 < CHUNKS:
-                add_bias(step - 3)
-                if step - 3 >= normed_chunks:
-                    store(step - 3, qkv[:, step - 3, :])
+            if 0 <= step - 1 < NORMED_PARTS:
+                bias_to_sbuf(step - 1)
+            if 0 <= step - 2 < CHUNKS:
+                add_bias(step - 2)
+                if step - 2 >= normed_chunks:
+                    store(step - 2, qkv[:, step - 2, :])
+            if 0 <= step - 3 < normed_chunks:
+                sum_the_squares(step - 3)
+                root(step - 3)
             if 0 <= step - 4 < normed_chunks:
-                sum_the_squares(step - 4)
-                root(step - 4)
-            if 0 <= step - 5 < normed_chunks:
-                normalise(step - 5)
-                store(step - 5, normed[:, step - 5, :])
+                normalise(step - 4)
+                store(step - 4, normed[:, step - 4, :])

@@ -45,10 +45,13 @@ FRESH_BANKS = 2
 FLOPS = 2 * P * K * PARTS * PART
 
 
+RUN = 2
+
+
 def runs_of_four(rows_first, columns_first):
     return (
-        columns_first.rearrange("p (g i) j -> p g j i", i=4),
-        rows_first.rearrange("p j (g i) -> p g j i", i=4),
+        columns_first.rearrange("p (g i) j -> p g j i", i=RUN),
+        rows_first.rearrange("p j (g i) -> p g j i", i=RUN),
     )
 
 

@@ -22,33 +22,24 @@ NORMED_PARTS = 2
 CHUNK = 512
 CHUNKS = PARTS * PART // CHUNK
 CHUNKS_PER_PART = PART // CHUNK
+NORMED_CHUNKS = NORMED_PARTS * CHUNKS_PER_PART
 HEADS_PER_CHUNK = CHUNK // HEAD
 EPS = 1e-6
 
 WINDOWS = 2
 WINDOW_W = 4
 
-SCALAR_COLS_FIRST = 192
-SCALAR_COLS_STEP = 32
-SCALAR_COLS_LAST = 352
+SCALAR_COLS = [256 - 32 * c for c in range(CHUNKS)]
 
+RUN = 2
 
-def scalar_cols(c):
-    return min(SCALAR_COLS_FIRST + SCALAR_COLS_STEP * c, SCALAR_COLS_LAST)
-
-ROW = 2 * HEAD
-ROWS_PER_PART = PART // ROW
-BIAS_ROWS = NORMED_PARTS * ROWS_PER_PART
-USED_ROWS = 16
-FRESH_BANKS = 2
+BIAS_ROWS = NORMED_PARTS * HEADS
+USED_ROWS = BIAS_ROWS + NORMED_PARTS
 
 FLOPS = 2 * P * K * PARTS * PART
 
 
-RUN = 2
-
-
-def runs_of_four(rows_first, columns_first):
+def runs_of_columns(rows_first, columns_first):
     return (
         columns_first.rearrange("p (g i) j -> p g j i", i=RUN),
         rows_first.rearrange("p j (g i) -> p g j i", i=RUN),
@@ -75,43 +66,46 @@ def tile_naswinattention_pa_s_kernel(
         w_grouped = keep.tile([P, CHUNKS, CHUNK, PACK], BF16, align_bytes=64)
         w_codes = keep.tile([P, CHUNKS, CHUNK], U32, align_bytes=64)
         w_scales = keep.tile([P, CHUNKS, CHUNK], U8, align_bytes=64)
-        bias = keep.tile([P, CHUNKS, CHUNK], BF16)
-        rows = keep.tile([P, ROW], BF16)
+        v_bias = keep.tile([P, CHUNKS_PER_PART, CHUNK], BF16)
+        rows = keep.tile([P, P], BF16)
         columns = keep.tile([P, USED_ROWS], F32)
-        qkv = keep.tile([P, CHUNKS, CHUNK], F32)
-        squares = keep.tile([P, NORMED_PARTS * PART], F32)
-        normed = keep.tile([P, NORMED_PARTS * CHUNKS_PER_PART, CHUNK], F32)
-        sum_squares = keep.tile([P, NORMED_PARTS * HEADS], F32)
-        inv_rms = keep.tile([P, NORMED_PARTS * HEADS], F32)
+        gains = keep.tile([P, NORMED_PARTS, HEAD], F32)
+        biased = keep.tile([P, NORMED_CHUNKS, CHUNK], F32)
+        squares = keep.tile([P, NORMED_CHUNKS, CHUNK], F32)
+        sum_squares = keep.tile([P, BIAS_ROWS], F32)
+        inv_rms = keep.tile([P, BIAS_ROWS], F32)
+        results = keep.tile([P, CHUNKS, CHUNK], F32)
         eps = keep.tile([P, 1], F32)
         table_warm = keep.tile([P, 1], F32)
         identity = keep.tile([P, P], F32)
+        identity_bf = keep.tile([P, P], BF16)
         to_windows = keep.tile([P, P], F32)
-        accs = [psum.tile([P, CHUNK], F32, name="acc%d" % c) for c in range(FRESH_BANKS)]
-        columns_ps = psum.tile([P, P], F32, name="acc%d" % FRESH_BANKS)
-        spread_bias = [
-            psum.tile([P, ROWS_PER_PART, P], F32, name="acc%d" % (FRESH_BANKS + 1 + part))
-            for part in range(NORMED_PARTS)
-        ]
-        gain_words = psum.tile([P, P], F32)
-        gains = gain_words[:].bitcast(BF16).rearrange("p (g f) -> p g f", g=NORMED_PARTS)
+
+        BANKS = 3
+        vid_t = psum.tile([P, 2, P], F32, name="v0")
+        columns_ps = psum.tile([P, P], BF16, name="turned2")
+        gains_ps = psum.tile([P, NORMED_PARTS, HEAD], F32, name="v1")
+        products = {}
+        turned = {}
 
         ctx.enter_context(tc.manual_schedule())
 
         nc.gpsimd.memset(rows[:], 0.0)
-        bias_rows = bqkv_vid.rearrange("(r f) -> r f", f=ROW)
         for c in range(CHUNKS):
             nc.sync.dma_start(out=w_raw[:, c], in_=w_rows[:, :, c * CHUNK : (c + 1) * CHUNK])
             if c == 0:
-                nc.sync.dma_start(out=rows[0:BIAS_ROWS, :], in_=bias_rows[0:BIAS_ROWS, :])
+                nc.sync.dma_start(out=vid_sb[:], in_=vid)
+                nc.sync.dma_start(
+                    out=rows[0:BIAS_ROWS, :],
+                    in_=bqkv_vid.rearrange("(r f) -> r f", f=HEAD)[0:BIAS_ROWS, :],
+                )
                 for part in range(NORMED_PARTS):
                     nc.sync.dma_start(
-                        out=rows[BIAS_ROWS : BIAS_ROWS + 1, part * HEAD : (part + 1) * HEAD],
+                        out=rows[BIAS_ROWS + part : BIAS_ROWS + part + 1, :],
                         in_=gain_rows[part].rearrange("(o f) -> o f", o=1),
                     )
-                nc.sync.dma_start(out=vid_sb[:], in_=vid)
         nc.sync.dma_start(
-            out=bias[:, NORMED_PARTS * CHUNKS_PER_PART : CHUNKS, :].rearrange("p c w -> p (c w)"),
+            out=v_bias[:].rearrange("p c w -> p (c w)"),
             in_=bqkv_vid[NORMED_PARTS * PART : PARTS * PART].partition_broadcast(P),
         )
 
@@ -124,31 +118,10 @@ def tile_naswinattention_pa_s_kernel(
             in_=identity[:].rearrange("l (r n c) -> l n r c", n=WINDOWS, c=WINDOW_W),
         )
 
-        def rows_to_columns():
-            nc.tensor.transpose(columns_ps[:], rows[:].bitcast(F32), identity[:])
-            nc.vector.tensor_copy(out=columns[:], in_=columns_ps[:, 0:USED_ROWS])
-
-        def spread(r, target):
-            nc.tensor.transpose(target, columns[:, r : r + 1].to_broadcast([P, P]), identity[:])
-
-        def spread_bias_of(part):
-            for i in range(ROWS_PER_PART):
-                spread(part * ROWS_PER_PART + i, spread_bias[part][:, i, :])
-
-        def spread_gains():
-            spread(BIAS_ROWS, gain_words[:])
-
-        def bias_to_sbuf(part):
-            nc.scalar.copy(
-                out=bias[:, part * CHUNKS_PER_PART : (part + 1) * CHUNKS_PER_PART, :]
-                .rearrange("p c w -> p (c w)")
-                .bitcast(F32),
-                in_=spread_bias[part][:].rearrange("p i w -> p (i w)"),
-            )
+        nc.vector.tensor_copy(out=identity_bf[:], in_=identity[:])
 
         def quantise_vid():
             vid_words = vid_sb[:].bitcast(F32).rearrange("l (p u) -> l u p", u=2)
-            vid_t = psum.tile([P, 2, P], F32)
             for u in range(2):
                 nc.tensor.transpose(vid_t[:, u, :], vid_words[:, u, :], to_windows[:])
             nc.vector.tensor_copy(
@@ -159,11 +132,21 @@ def tile_naswinattention_pa_s_kernel(
                 out=vid_codes[:].bitcast(FP8X4), scales=vid_scales[:], in_=vid_grouped[:]
             )
 
+        def bias_and_gains():
+            nc.tensor.transpose(columns_ps[:], rows[:], identity_bf[:])
+            nc.vector.tensor_copy(out=columns[:], in_=columns_ps[:, 0:USED_ROWS])
+
+        def spread_gains():
+            for part in range(NORMED_PARTS):
+                column = columns[:, BIAS_ROWS + part : BIAS_ROWS + part + 1]
+                nc.tensor.transpose(gains_ps[:, part, :], column.to_broadcast([P, P]), identity[:])
+            nc.scalar.copy(out=gains[:], in_=gains_ps[:])
+
         def regroup(c):
-            cut = scalar_cols(c)
-            dst, src = runs_of_four(w_raw[:, c, :, 0:cut], w_grouped[:, c, 0:cut, :])
+            cut = SCALAR_COLS[c]
+            dst, src = runs_of_columns(w_raw[:, c, :, 0:cut], w_grouped[:, c, 0:cut, :])
             nc.scalar.copy(out=dst, in_=src)
-            dst, src = runs_of_four(w_raw[:, c, :, cut:CHUNK], w_grouped[:, c, cut:CHUNK, :])
+            dst, src = runs_of_columns(w_raw[:, c, :, cut:CHUNK], w_grouped[:, c, cut:CHUNK, :])
             nc.vector.tensor_copy(out=dst, in_=src)
 
         def quantise(c):
@@ -174,39 +157,58 @@ def tile_naswinattention_pa_s_kernel(
             )
 
         def project(c):
-            if c >= FRESH_BANKS:
-                accs.append(psum.tile([P, CHUNK], F32, name="acc%d" % c))
-            nc.tensor.matmul_mx(
-                out=accs[c][:],
-                lhsT=vid_codes[:].bitcast(FP8X4),
-                lhsT_scale=vid_scales[:],
-                rhs=w_codes[:, c, :].bitcast(FP8X4),
-                rhs_scale=w_scales[:, c, :],
-                start=True,
-                stop=True,
-            )
+            if c >= NORMED_CHUNKS:
+                products[c] = psum.tile([P, CHUNK], F32, name="v%d" % (c - NORMED_CHUNKS))
+                nc.tensor.matmul_mx(
+                    out=products[c][:],
+                    lhsT=vid_codes[:].bitcast(FP8X4),
+                    lhsT_scale=vid_scales[:],
+                    rhs=w_codes[:, c, :].bitcast(FP8X4),
+                    rhs_scale=w_scales[:, c, :],
+                    start=True,
+                    stop=True,
+                )
+                return
+            products[c] = psum.tile([P, CHUNK], F32, name="product%d" % (c % BANKS))
+            for h in range(HEADS_PER_CHUNK):
+                features = slice(h * HEAD, (h + 1) * HEAD)
+                nc.tensor.matmul_mx(
+                    out=products[c][:, features],
+                    lhsT=w_codes[:, c, features].bitcast(FP8X4),
+                    lhsT_scale=w_scales[:, c, features],
+                    rhs=vid_codes[:].bitcast(FP8X4),
+                    rhs_scale=vid_scales[:],
+                    start=True,
+                    stop=True,
+                )
 
         def add_bias(c):
-            nc.vector.tensor_tensor(
-                out=qkv[:, c, :], in0=accs[c][:], in1=bias[:, c, :], op=ALU.add
-            )
+            for h in range(HEADS_PER_CHUNK):
+                head = c * HEADS_PER_CHUNK + h
+                tokens = slice(h * P, (h + 1) * P)
+                nc.scalar.activation(
+                    out=biased[:, c, tokens],
+                    in_=products[c][:, tokens],
+                    func=ACT.Identity,
+                    bias=columns[:, head : head + 1],
+                )
 
-        def store(c, result):
-            part = c // CHUNKS_PER_PART
-            first = (c % CHUNKS_PER_PART) * CHUNK
-            nc.sync.dma_start(out=out_rows[part][:, first : first + CHUNK], in_=result)
+        def turn(c):
+            turned[c] = psum.tile([P, CHUNK], F32, name="turned%d" % (c % BANKS))
+            for h in range(HEADS_PER_CHUNK):
+                block = slice(h * P, (h + 1) * P)
+                nc.tensor.transpose(turned[c][:, block], biased[:, c, block], identity[:])
 
         def sum_the_squares(c):
             for h in range(HEADS_PER_CHUNK):
                 head = c * HEADS_PER_CHUNK + h
+                features = slice(h * HEAD, (h + 1) * HEAD)
                 nc.scalar.activation(
-                    out=squares[:, head * HEAD : (head + 1) * HEAD],
-                    in_=qkv[:, c, h * HEAD : (h + 1) * HEAD],
+                    out=squares[:, c, features],
+                    in_=turned[c][:, features],
                     func=ACT.Square,
                     accum_out=sum_squares[:, head : head + 1],
                 )
-
-        def root(c):
             heads = slice(c * HEADS_PER_CHUNK, (c + 1) * HEADS_PER_CHUNK)
             nc.scalar.activation(
                 out=inv_rms[:, heads],
@@ -221,36 +223,51 @@ def tile_naswinattention_pa_s_kernel(
                 head = c * HEADS_PER_CHUNK + h
                 features = slice(h * HEAD, (h + 1) * HEAD)
                 nc.vector.scalar_tensor_tensor(
-                    out=normed[:, c, features],
-                    in0=qkv[:, c, features],
+                    out=results[:, c, features],
+                    in0=turned[c][:, features],
                     scalar=inv_rms[:, head : head + 1],
                     in1=gains[:, c // CHUNKS_PER_PART, :],
                     op0=ALU.mult,
                     op1=ALU.mult,
                 )
 
-        normed_chunks = NORMED_PARTS * CHUNKS_PER_PART
-        for step in range(CHUNKS + 2):
-            if 0 <= step - 1 < CHUNKS:
-                quantise(step - 1)
-                project(step - 1)
-            if step < CHUNKS:
-                regroup(step)
-            if step == 0:
-                rows_to_columns()
-                quantise_vid()
-                for part in range(NORMED_PARTS):
-                    spread_bias_of(part)
+        def add_v_bias(c):
+            nc.vector.tensor_tensor(
+                out=results[:, c, :],
+                in0=products[c][:],
+                in1=v_bias[:, c - NORMED_CHUNKS, :],
+                op=ALU.add,
+            )
+
+        def store(c):
+            part = c // CHUNKS_PER_PART
+            first = (c % CHUNKS_PER_PART) * CHUNK
+            nc.sync.dma_start(out=out_rows[part][:, first : first + CHUNK], in_=results[:, c, :])
+
+        regroup(0)
+        quantise_vid()
+        bias_and_gains()
+        quantise(0)
+        project(0)
+        regroup(1)
+        regroup(2)
+        for c in range(1, CHUNKS + 1):
+            if c - 1 < NORMED_CHUNKS:
+                add_bias(c - 1)
+            if c == 1:
                 spread_gains()
-            if 0 <= step - 1 < NORMED_PARTS:
-                bias_to_sbuf(step - 1)
-            if 0 <= step - 2 < CHUNKS:
-                add_bias(step - 2)
-                if step - 2 >= normed_chunks:
-                    store(step - 2, qkv[:, step - 2, :])
-            if 0 <= step - 3 < normed_chunks:
-                sum_the_squares(step - 3)
-                root(step - 3)
-            if 0 <= step - 4 < normed_chunks:
-                normalise(step - 4)
-                store(step - 4, normed[:, step - 4, :])
+            if 0 <= c - 2 < NORMED_CHUNKS:
+                sum_the_squares(c - 2)
+            if c < CHUNKS:
+                quantise(c)
+                project(c)
+            if c - 1 < NORMED_CHUNKS:
+                turn(c - 1)
+            else:
+                add_v_bias(c - 1)
+                store(c - 1)
+            if 0 <= c - 3 < NORMED_CHUNKS:
+                normalise(c - 3)
+                store(c - 3)
+            if c + 2 < CHUNKS:
+                regroup(c + 2)

@@ -29,7 +29,7 @@ EPS = 1e-6
 WINDOWS = 2
 WINDOW_W = 4
 
-SCALAR_COLS = [256 - 32 * c for c in range(CHUNKS)]
+SCALAR_COLS = [288 - 48 * c for c in range(CHUNKS)]
 
 RUN = 2
 
@@ -81,9 +81,9 @@ def tile_naswinattention_pa_s_kernel(
         identity_bf = keep.tile([P, P], BF16)
         to_windows = keep.tile([P, P], F32)
 
-        BANKS = 3
+        PRODUCT_BANKS = 2
         vid_t = psum.tile([P, 2, P], F32, name="v0")
-        columns_ps = psum.tile([P, P], BF16, name="turned2")
+        columns_ps = psum.tile([P, P], BF16, name="turned3")
         gains_ps = psum.tile([P, NORMED_PARTS, HEAD], F32, name="v1")
         products = {}
         turned = {}
@@ -169,7 +169,7 @@ def tile_naswinattention_pa_s_kernel(
                     stop=True,
                 )
                 return
-            products[c] = psum.tile([P, CHUNK], F32, name="product%d" % (c % BANKS))
+            products[c] = psum.tile([P, CHUNK], F32, name="product%d" % (c % PRODUCT_BANKS))
             for h in range(HEADS_PER_CHUNK):
                 features = slice(h * HEAD, (h + 1) * HEAD)
                 nc.tensor.matmul_mx(
@@ -194,7 +194,7 @@ def tile_naswinattention_pa_s_kernel(
                 )
 
         def turn(c):
-            turned[c] = psum.tile([P, CHUNK], F32, name="turned%d" % (c % BANKS))
+            turned[c] = psum.tile([P, CHUNK], F32, name="turned%d" % c)
             for h in range(HEADS_PER_CHUNK):
                 block = slice(h * P, (h + 1) * P)
                 nc.tensor.transpose(turned[c][:, block], biased[:, c, block], identity[:])
@@ -251,23 +251,23 @@ def tile_naswinattention_pa_s_kernel(
         project(0)
         regroup(1)
         regroup(2)
-        for c in range(1, CHUNKS + 1):
+        for c in range(1, CHUNKS + 2):
             if c - 1 < NORMED_CHUNKS:
                 add_bias(c - 1)
             if c == 1:
                 spread_gains()
-            if 0 <= c - 2 < NORMED_CHUNKS:
-                sum_the_squares(c - 2)
+            if 0 <= c - 3 < NORMED_CHUNKS:
+                sum_the_squares(c - 3)
             if c < CHUNKS:
                 quantise(c)
                 project(c)
             if c - 1 < NORMED_CHUNKS:
                 turn(c - 1)
-            else:
+            elif c - 1 < CHUNKS:
                 add_v_bias(c - 1)
                 store(c - 1)
-            if 0 <= c - 3 < NORMED_CHUNKS:
-                normalise(c - 3)
-                store(c - 3)
+            if 0 <= c - 4 < NORMED_CHUNKS:
+                normalise(c - 4)
+                store(c - 4)
             if c + 2 < CHUNKS:
                 regroup(c + 2)

@@ -29,12 +29,11 @@ EPS = 1e-6
 WINDOWS = 2
 WINDOW_W = 4
 
-SCALAR_COLS = [288 - 48 * c for c in range(CHUNKS)]
+SCALAR_COLS = [208] + [304 - 48 * c for c in range(1, CHUNKS)]
 
 RUN = 2
 
 BIAS_ROWS = NORMED_PARTS * HEADS
-USED_ROWS = BIAS_ROWS + NORMED_PARTS
 
 FLOPS = 2 * P * K * PARTS * PART
 
@@ -68,8 +67,8 @@ def tile_naswinattention_pa_s_kernel(
         w_scales = keep.tile([P, CHUNKS, CHUNK], U8, align_bytes=64)
         v_bias = keep.tile([P, CHUNKS_PER_PART, CHUNK], BF16)
         rows = keep.tile([P, P], BF16)
-        columns = keep.tile([P, USED_ROWS], F32)
-        gains = keep.tile([P, NORMED_PARTS, HEAD], F32)
+        columns = keep.tile([P, BIAS_ROWS], F32)
+        gains = keep.tile([P, NORMED_PARTS, HEAD], BF16)
         biased = keep.tile([P, NORMED_CHUNKS, CHUNK], F32)
         squares = keep.tile([P, NORMED_CHUNKS, CHUNK], F32)
         sum_squares = keep.tile([P, BIAS_ROWS], F32)
@@ -84,26 +83,22 @@ def tile_naswinattention_pa_s_kernel(
         PRODUCT_BANKS = 2
         vid_t = psum.tile([P, 2, P], F32, name="v0")
         columns_ps = psum.tile([P, P], BF16, name="turned3")
-        gains_ps = psum.tile([P, NORMED_PARTS, HEAD], F32, name="v1")
         products = {}
         turned = {}
 
         ctx.enter_context(tc.manual_schedule())
 
         nc.gpsimd.memset(rows[:], 0.0)
+        nc.sync.dma_start(out=vid_sb[:], in_=vid)
         for c in range(CHUNKS):
             nc.sync.dma_start(out=w_raw[:, c], in_=w_rows[:, :, c * CHUNK : (c + 1) * CHUNK])
             if c == 0:
-                nc.sync.dma_start(out=vid_sb[:], in_=vid)
                 nc.sync.dma_start(
                     out=rows[0:BIAS_ROWS, :],
                     in_=bqkv_vid.rearrange("(r f) -> r f", f=HEAD)[0:BIAS_ROWS, :],
                 )
-                for part in range(NORMED_PARTS):
-                    nc.sync.dma_start(
-                        out=rows[BIAS_ROWS + part : BIAS_ROWS + part + 1, :],
-                        in_=gain_rows[part].rearrange("(o f) -> o f", o=1),
-                    )
+        for part in range(NORMED_PARTS):
+            nc.sync.dma_start(out=gains[:, part, :], in_=gain_rows[part].partition_broadcast(P))
         nc.sync.dma_start(
             out=v_bias[:].rearrange("p c w -> p (c w)"),
             in_=bqkv_vid[NORMED_PARTS * PART : PARTS * PART].partition_broadcast(P),
@@ -120,7 +115,7 @@ def tile_naswinattention_pa_s_kernel(
 
         nc.vector.tensor_copy(out=identity_bf[:], in_=identity[:])
 
-        def quantise_vid():
+        def turn_vid():
             vid_words = vid_sb[:].bitcast(F32).rearrange("l (p u) -> l u p", u=2)
             for u in range(2):
                 nc.tensor.transpose(vid_t[:, u, :], vid_words[:, u, :], to_windows[:])
@@ -128,19 +123,15 @@ def tile_naswinattention_pa_s_kernel(
                 out=vid_grouped[:].bitcast(F32).rearrange("p (l u) -> p l u", u=2),
                 in_=vid_t[:].rearrange("p u l -> p l u"),
             )
+
+        def quantise_vid():
             nc.vector.quantize_mx(
                 out=vid_codes[:].bitcast(FP8X4), scales=vid_scales[:], in_=vid_grouped[:]
             )
 
-        def bias_and_gains():
+        def bias_columns():
             nc.tensor.transpose(columns_ps[:], rows[:], identity_bf[:])
-            nc.vector.tensor_copy(out=columns[:], in_=columns_ps[:, 0:USED_ROWS])
-
-        def spread_gains():
-            for part in range(NORMED_PARTS):
-                column = columns[:, BIAS_ROWS + part : BIAS_ROWS + part + 1]
-                nc.tensor.transpose(gains_ps[:, part, :], column.to_broadcast([P, P]), identity[:])
-            nc.scalar.copy(out=gains[:], in_=gains_ps[:])
+            nc.vector.tensor_copy(out=columns[:], in_=columns_ps[:, 0:BIAS_ROWS])
 
         def regroup(c):
             cut = SCALAR_COLS[c]
@@ -244,9 +235,10 @@ def tile_naswinattention_pa_s_kernel(
             first = (c % CHUNKS_PER_PART) * CHUNK
             nc.sync.dma_start(out=out_rows[part][:, first : first + CHUNK], in_=results[:, c, :])
 
+        turn_vid()
         regroup(0)
         quantise_vid()
-        bias_and_gains()
+        bias_columns()
         quantise(0)
         project(0)
         regroup(1)
@@ -254,8 +246,6 @@ def tile_naswinattention_pa_s_kernel(
         for c in range(1, CHUNKS + 2):
             if c - 1 < NORMED_CHUNKS:
                 add_bias(c - 1)
-            if c == 1:
-                spread_gains()
             if 0 <= c - 3 < NORMED_CHUNKS:
                 sum_the_squares(c - 3)
             if c < CHUNKS:

from contextlib import ExitStack

import concourse.mybir as mybir
from concourse.masks import make_identity

F32 = mybir.dt.float32
BF16 = mybir.dt.bfloat16
U32 = mybir.dt.uint32
U8 = mybir.dt.uint8
FP8X4 = mybir.dt.float8_e4m3fn_x4
ALU = mybir.AluOpType
ACT = mybir.ActivationFunctionType

P = 128
PACK = 4
K = P * PACK
HEAD = 128
HEADS = 8
PART = HEADS * HEAD
PARTS = 3
NORMED_PARTS = 2
CHUNK = 512
CHUNKS = PARTS * PART // CHUNK
CHUNKS_PER_PART = PART // CHUNK
NORMED_CHUNKS = NORMED_PARTS * CHUNKS_PER_PART
HEADS_PER_CHUNK = CHUNK // HEAD
EPS = 1e-6

WINDOWS = 2
WINDOW_W = 4

SCALAR_COLS = [208] + [304 - 48 * c for c in range(1, CHUNKS)]

RUN = 2

BIAS_ROWS = NORMED_PARTS * HEADS

FLOPS = 2 * P * K * PARTS * PART


def runs_of_columns(rows_first, columns_first):
    return (
        columns_first.rearrange("p (g i) j -> p g j i", i=RUN),
        rows_first.rearrange("p j (g i) -> p g j i", i=RUN),
    )


def tile_naswinattention_pa_s_kernel(
    tc, vid, Wqkv_vid, bqkv_vid, q_scale_vid, k_scale_vid, out_0, out_1, out_2
):
    nc = tc.nc
    out_rows = [o.rearrange("n p h f -> (n p) (h f)") for o in (out_0, out_1, out_2)]
    w_rows = Wqkv_vid.rearrange("(p j) n -> p j n", j=PACK)
    gain_rows = [q_scale_vid, k_scale_vid]

    with ExitStack() as ctx:
        keep = ctx.enter_context(tc.tile_pool(name="keep", bufs=1))
        psum = ctx.enter_context(tc.psum_pool(name="psum", bufs=1))

        vid_sb = keep.tile([P, K], BF16)
        vid_grouped = keep.tile([P, P * PACK], BF16, align_bytes=64)
        vid_codes = keep.tile([P, P], U32, align_bytes=64)
        vid_scales = keep.tile([P, P], U8, align_bytes=64)
        w_raw = keep.tile([P, CHUNKS, PACK, CHUNK], BF16)
        w_grouped = keep.tile([P, CHUNKS, CHUNK, PACK], BF16, align_bytes=64)
        w_codes = keep.tile([P, CHUNKS, CHUNK], U32, align_bytes=64)
        w_scales = keep.tile([P, CHUNKS, CHUNK], U8, align_bytes=64)
        v_bias = keep.tile([P, CHUNKS_PER_PART, CHUNK], BF16)
        rows = keep.tile([P, P], BF16)
        columns = keep.tile([P, BIAS_ROWS], F32)
        gains = keep.tile([P, NORMED_PARTS, HEAD], BF16)
        biased = keep.tile([P, NORMED_CHUNKS, CHUNK], F32)
        squares = keep.tile([P, NORMED_CHUNKS, CHUNK], F32)
        sum_squares = keep.tile([P, BIAS_ROWS], F32)
        inv_rms = keep.tile([P, BIAS_ROWS], F32)
        results = keep.tile([P, CHUNKS, CHUNK], F32)
        eps = keep.tile([P, 1], F32)
        table_warm = keep.tile([P, 1], F32)
        identity = keep.tile([P, P], F32)
        identity_bf = keep.tile([P, P], BF16)
        to_windows = keep.tile([P, P], F32)

        PRODUCT_BANKS = 2
        vid_t = psum.tile([P, 2, P], F32, name="v0")
        columns_ps = psum.tile([P, P], BF16, name="turned3")
        products = {}
        turned = {}

        ctx.enter_context(tc.manual_schedule())

        nc.gpsimd.memset(rows[:], 0.0)
        nc.sync.dma_start(out=vid_sb[:], in_=vid)
        for c in range(CHUNKS):
            nc.sync.dma_start(out=w_raw[:, c], in_=w_rows[:, :, c * CHUNK : (c + 1) * CHUNK])
            if c == 0:
                nc.sync.dma_start(
                    out=rows[0:BIAS_ROWS, :],
                    in_=bqkv_vid.rearrange("(r f) -> r f", f=HEAD)[0:BIAS_ROWS, :],
                )
        for part in range(NORMED_PARTS):
            nc.sync.dma_start(out=gains[:, part, :], in_=gain_rows[part].partition_broadcast(P))
        nc.sync.dma_start(
            out=v_bias[:].rearrange("p c w -> p (c w)"),
            in_=bqkv_vid[NORMED_PARTS * PART : PARTS * PART].partition_broadcast(P),
        )

        nc.vector.memset(eps[:], EPS)
        nc.scalar.activation(out=table_warm[:], in_=eps[:], func=ACT.Abs_reciprocal_sqrt)

        make_identity(nc, identity[:])
        nc.vector.tensor_copy(
            out=to_windows[:].rearrange("l (n r c) -> l n r c", n=WINDOWS, c=WINDOW_W),
            in_=identity[:].rearrange("l (r n c) -> l n r c", n=WINDOWS, c=WINDOW_W),
        )

        nc.vector.tensor_copy(out=identity_bf[:], in_=identity[:])

        def turn_vid():
            vid_words = vid_sb[:].bitcast(F32).rearrange("l (p u) -> l u p", u=2)
            for u in range(2):
                nc.tensor.transpose(vid_t[:, u, :], vid_words[:, u, :], to_windows[:])
            nc.vector.tensor_copy(
                out=vid_grouped[:].bitcast(F32).rearrange("p (l u) -> p l u", u=2),
                in_=vid_t[:].rearrange("p u l -> p l u"),
            )

        def quantise_vid():
            nc.vector.quantize_mx(
                out=vid_codes[:].bitcast(FP8X4), scales=vid_scales[:], in_=vid_grouped[:]
            )

        def bias_columns():
            nc.tensor.transpose(columns_ps[:], rows[:], identity_bf[:])
            nc.vector.tensor_copy(out=columns[:], in_=columns_ps[:, 0:BIAS_ROWS])

        def regroup(c):
            cut = SCALAR_COLS[c]
            dst, src = runs_of_columns(w_raw[:, c, :, 0:cut], w_grouped[:, c, 0:cut, :])
            nc.scalar.copy(out=dst, in_=src)
            dst, src = runs_of_columns(w_raw[:, c, :, cut:CHUNK], w_grouped[:, c, cut:CHUNK, :])
            nc.vector.tensor_copy(out=dst, in_=src)

        def quantise(c):
            nc.vector.quantize_mx(
                out=w_codes[:, c, :].bitcast(FP8X4),
                scales=w_scales[:, c, :],
                in_=w_grouped[:, c].rearrange("p w j -> p (w j)"),
            )

        def project(c):
            if c >= NORMED_CHUNKS:
                products[c] = psum.tile([P, CHUNK], F32, name="v%d" % (c - NORMED_CHUNKS))
                nc.tensor.matmul_mx(
                    out=products[c][:],
                    lhsT=vid_codes[:].bitcast(FP8X4),
                    lhsT_scale=vid_scales[:],
                    rhs=w_codes[:, c, :].bitcast(FP8X4),
                    rhs_scale=w_scales[:, c, :],
                    start=True,
                    stop=True,
                )
                return
            products[c] = psum.tile([P, CHUNK], F32, name="product%d" % (c % PRODUCT_BANKS))
            for h in range(HEADS_PER_CHUNK):
                features = slice(h * HEAD, (h + 1) * HEAD)
                nc.tensor.matmul_mx(
                    out=products[c][:, features],
                    lhsT=w_codes[:, c, features].bitcast(FP8X4),
                    lhsT_scale=w_scales[:, c, features],
                    rhs=vid_codes[:].bitcast(FP8X4),
                    rhs_scale=vid_scales[:],
                    start=True,
                    stop=True,
                )

        def add_bias(c):
            for h in range(HEADS_PER_CHUNK):
                head = c * HEADS_PER_CHUNK + h
                tokens = slice(h * P, (h + 1) * P)
                nc.scalar.activation(
                    out=biased[:, c, tokens],
                    in_=products[c][:, tokens],
                    func=ACT.Identity,
                    bias=columns[:, head : head + 1],
                )

        def turn(c):
            turned[c] = psum.tile([P, CHUNK], F32, name="turned%d" % c)
            for h in range(HEADS_PER_CHUNK):
                block = slice(h * P, (h + 1) * P)
                nc.tensor.transpose(turned[c][:, block], biased[:, c, block], identity[:])

        def sum_the_squares(c):
            for h in range(HEADS_PER_CHUNK):
                head = c * HEADS_PER_CHUNK + h
                features = slice(h * HEAD, (h + 1) * HEAD)
                nc.scalar.activation(
                    out=squares[:, c, features],
                    in_=turned[c][:, features],
                    func=ACT.Square,
                    accum_out=sum_squares[:, head : head + 1],
                )
            heads = slice(c * HEADS_PER_CHUNK, (c + 1) * HEADS_PER_CHUNK)
            nc.scalar.activation(
                out=inv_rms[:, heads],
                in_=sum_squares[:, heads],
                func=ACT.Abs_reciprocal_sqrt,
                bias=eps[:],
                scale=1.0 / HEAD,
            )

        def normalise(c):
            for h in range(HEADS_PER_CHUNK):
                head = c * HEADS_PER_CHUNK + h
                features = slice(h * HEAD, (h + 1) * HEAD)
                nc.vector.scalar_tensor_tensor(
                    out=results[:, c, features],
                    in0=turned[c][:, features],
                    scalar=inv_rms[:, head : head + 1],
                    in1=gains[:, c // CHUNKS_PER_PART, :],
                    op0=ALU.mult,
                    op1=ALU.mult,
                )

        def add_v_bias(c):
            nc.vector.tensor_tensor(
                out=results[:, c, :],
                in0=products[c][:],
                in1=v_bias[:, c - NORMED_CHUNKS, :],
                op=ALU.add,
            )

        def store(c):
            part = c // CHUNKS_PER_PART
            first = (c % CHUNKS_PER_PART) * CHUNK
            nc.sync.dma_start(out=out_rows[part][:, first : first + CHUNK], in_=results[:, c, :])

        turn_vid()
        regroup(0)
        quantise_vid()
        bias_columns()
        quantise(0)
        project(0)
        regroup(1)
        regroup(2)
        for c in range(1, CHUNKS + 2):
            if c - 1 < NORMED_CHUNKS:
                add_bias(c - 1)
            if 0 <= c - 3 < NORMED_CHUNKS:
                sum_the_squares(c - 3)
            if c < CHUNKS:
                quantise(c)
                project(c)
            if c - 1 < NORMED_CHUNKS:
                turn(c - 1)
            elif c - 1 < CHUNKS:
                add_v_bias(c - 1)
                store(c - 1)
            if 0 <= c - 4 < NORMED_CHUNKS:
                normalise(c - 4)
                store(c - 4)
            if c + 2 < CHUNKS:
                regroup(c + 2)
